import numpy as np
import ml_dtypes


def mxq(x, axis, fmt="e4m3"):
    dtype, down = {"e4m3": (ml_dtypes.float8_e4m3fn, 7), "e5m2": (ml_dtypes.float8_e5m2, 14)}[fmt]
    v = np.moveaxis(np.asarray(x, np.float32).astype(ml_dtypes.bfloat16).astype(np.float64), axis, -1)
    blocks = v.reshape(v.shape[:-1] + (-1, 32))
    amax = np.abs(blocks).max(-1, keepdims=True)
    byte = np.maximum(np.where(amax > 0, np.frexp(amax)[1] - 1 + 127, 0) - down, 1)
    scale = np.exp2(byte - 127.0)
    codes = (blocks / scale).astype(np.float32).astype(dtype).astype(np.float64)
    return np.moveaxis((codes * scale).reshape(v.shape), -1, axis)


WIDE = False


def mx_kscale(k):
    if not WIDE:
        return np.ones(k)
    levels = np.array([10, -10, 5, -5, 0])
    a = np.random.permutation(np.resize(levels, k // 512 * 4)).reshape(k // 512, 4)
    idx = np.arange(k)
    return np.exp2(a[idx // 512, idx % 128 // 32])


BF16 = ml_dtypes.bfloat16


def bf(x):
    return np.asarray(x, np.float32).astype(BF16)


def f64(x):
    return np.asarray(x).astype(np.float64)


B, S, D, E, HD = 4, 1024, 512, 1024, 64
ROPE_BASE = 10000.0


def rope_tables():
    inv_freq = 1.0 / ROPE_BASE ** (np.arange(0, E, 2) / E)
    ang = np.repeat(np.arange(S)[:, None] * inv_freq[None, :], 2, axis=-1)
    return np.cos(ang), np.sin(ang)


def rotate_half(v):
    h = v.shape[-1] // 2
    return np.concatenate([-v[..., h:], v[..., :h]], axis=-1)


def setup_inputs():
    s = mx_kscale(D)
    return {"x": bf(np.random.standard_normal((B, S, D)) * s),
            "Wq": bf(np.random.standard_normal((D, E)) * 0.5 / np.sqrt(D) / s[:, None]),
            "bq": bf(np.random.standard_normal(E) * 0.1),
            "Wk": bf(np.random.standard_normal((D, E)) * 0.5 / np.sqrt(D) / s[:, None]),
            "bk": bf(np.random.standard_normal(E) * 0.1)}


def reference(x, Wq, bq, Wk, bk):
    xq = mxq(f64(x), 2, "e4m3")
    q = (xq @ mxq(f64(Wq), 0, "e4m3")) + f64(bq)
    k = (xq @ mxq(f64(Wk), 0, "e4m3")) + f64(bk)
    cos, sin = rope_tables()
    qr = q * cos + rotate_half(q) * sin
    kr = k * cos + rotate_half(k) * sin
    return qr, kr

@@ -1,0 +1,256 @@
+from contextlib import ExitStack
+
+import concourse.masks as masks
+import concourse.mybir as mybir
+
+F32 = mybir.dt.float32
+BF16 = mybir.dt.bfloat16
+U32 = mybir.dt.uint32
+U8 = mybir.dt.uint8
+FP8X4 = mybir.dt.float8_e4m3fn_x4
+ALU = mybir.AluOpType
+ACT = mybir.ActivationFunctionType
+
+P = 128
+PACK = 4
+BATCH, SEQ, D_IN, D_OUT = 4, 1024, 512, 1024
+ROPE_BASE = 10000.0
+PI = 3.141592653589793
+assert D_IN == P * PACK
+
+N_BLOCKS = SEQ // P
+TOKENS = BATCH * P
+N_FT = D_OUT // P
+HALF_FT = N_FT // 2
+WORDS = D_IN // 2
+
+FREQ_STEP = ROPE_BASE ** (-2.0 / D_OUT)
+ROUND_MAGIC = 12582912.0
+
+FLOPS = 2 * BATCH * SEQ * D_IN * 2 * D_OUT
+
+
+def load_weight(nc, pool, w, label):
+    raw = pool.tile([P, PACK, D_OUT], BF16, name="raw_" + label)
+    for u in range(2):
+        nc.sync.dma_start(
+            out=raw[:, 2 * u : 2 * u + 2, :],
+            in_=w[u * 2 * P : (u + 1) * 2 * P, :].rearrange("(q e) c -> q e c", e=2),
+        )
+    return raw
+
+
+def quantise_weight(nc, pool, raw, label):
+    grouped = pool.tile([P, D_OUT, PACK], BF16, name="grouped_" + label, align_bytes=64)
+    nc.vector.tensor_copy(
+        out=grouped[:].rearrange("p (c i) t -> p c t i", i=4),
+        in_=raw[:].rearrange("p t (c i) -> p c t i", i=4),
+    )
+    codes = pool.tile([P, D_OUT], U32, name="codes_" + label, align_bytes=64)
+    scales = pool.tile([P, D_OUT], U8, name="scales_" + label, align_bytes=64)
+    nc.vector.quantize_mx(
+        out=codes[:].bitcast(FP8X4),
+        scales=scales[:],
+        in_=grouped[:].rearrange("p c t -> p (c t)"),
+    )
+    return codes, scales
+
+
+def tile_ropemultiheadattention_pa_t_kernel(tc, x, Wq, bq, Wk, bk, out_0, out_1):
+    nc = tc.nc
+    outs = (out_0, out_1)
+    with ExitStack() as ctx:
+        const = ctx.enter_context(tc.tile_pool(name="const", bufs=1))
+        xin_pool = ctx.enter_context(tc.tile_pool(name="xin", bufs=3))
+        xq_pool = ctx.enter_context(tc.tile_pool(name="xq", bufs=2))
+        angle_pool = ctx.enter_context(tc.tile_pool(name="angle", bufs=1))
+        table_pool = ctx.enter_context(tc.tile_pool(name="table", bufs=2))
+        prod_pool = ctx.enter_context(tc.tile_pool(name="prod", bufs=3))
+        stage_pool = ctx.enter_context(tc.tile_pool(name="stage", bufs=2))
+        mx_psum = ctx.enter_context(tc.psum_pool(name="mx_psum", bufs=4))
+        sum_psum = ctx.enter_context(tc.psum_pool(name="sum_psum", bufs=3))
+        xt_psum = ctx.enter_context(tc.psum_pool(name="xt_psum", bufs=1))
+
+        def load_x(t):
+            xin = xin_pool.tile([P, BATCH, D_IN], BF16, name="xin", tag="xin")
+            nc.sync.dma_start(
+                out=xin[:], in_=x[:, t * P : (t + 1) * P, :].rearrange("b p k -> p b k")
+            )
+            return xin
+
+        xin_next = load_x(0)
+        raw_q = load_weight(nc, const, Wq, "q")
+        bias_rows = const.tile([P, P], BF16, name="bias_rows")
+        nc.vector.memset(bias_rows[:], 0.0)
+        nc.sync.dma_start(out=bias_rows[0:N_FT, :], in_=bq.rearrange("(r c) -> r c", c=P))
+        nc.sync.dma_start(out=bias_rows[N_FT : 2 * N_FT, :], in_=bk.rearrange("(r c) -> r c", c=P))
+        raw_k = load_weight(nc, const, Wk, "k")
+
+        ident = const.tile([P, P], F32, name="ident")
+        masks.make_identity(nc, ident[:])
+
+        pos = const.tile([P, SEQ], F32, name="pos")
+        nc.vector.memset(pos[:, 0:1], 0.0)
+        w = 1
+        while w < SEQ:
+            nc.vector.tensor_scalar_add(out=pos[:, w : 2 * w], in0=pos[:, 0:w], scalar1=float(w))
+            w *= 2
+
+        step_row = const.tile([P, P], F32, name="step_row")
+        nc.vector.memset(step_row[:, 0:2], 1.0)
+        w = 2
+        while w < P:
+            nc.vector.tensor_scalar_mul(
+                out=step_row[:, w : 2 * w], in0=step_row[:, 0:w], scalar1=FREQ_STEP ** (w // 2)
+            )
+            w *= 2
+
+        bias_rows_f32 = const.tile([P, P], F32, name="bias_rows_f32")
+        nc.vector.tensor_copy(out=bias_rows_f32[:], in_=bias_rows[:])
+        setup = xt_psum.tile([P, 2, P], F32, name="setup", tag="xt")
+        nc.tensor.transpose(out=setup[:, 0, :], in_=bias_rows_f32[:], identity=ident[:])
+        nc.tensor.transpose(out=setup[:, 1, :], in_=step_row[:], identity=ident[:])
+        bias = const.tile([P, 2 * N_FT], F32, name="bias")
+        nc.vector.tensor_copy(out=bias[:], in_=setup[:, 0, 0 : 2 * N_FT])
+        turns = const.tile([P, N_FT], F32, name="turns")
+        nc.vector.tensor_scalar_mul(
+            out=turns[:, 0:1], in0=setup[:, 1, 0:1], scalar1=1.0 / (2.0 * PI)
+        )
+        w = 1
+        while w < N_FT:
+            nc.vector.tensor_scalar_mul(
+                out=turns[:, w : 2 * w], in0=turns[:, 0:w], scalar1=FREQ_STEP ** (w * P // 2)
+            )
+            w *= 2
+        half_pi = const.tile([P, 1], F32, name="half_pi")
+        nc.vector.memset(half_pi[:], 1.0)
+        nc.vector.tensor_scalar_mul(out=half_pi[:], in0=half_pi[:], scalar1=PI / 2.0)
+
+        def rope_tables(t):
+            shape = [P, N_FT, P]
+            angle = angle_pool.tile(shape, F32, name="angle", tag="angle")
+            nc.gpsimd.tensor_tensor(
+                out=angle[:],
+                in0=pos[:, t * P : (t + 1) * P].unsqueeze(1).to_broadcast(shape),
+                in1=turns[:].unsqueeze(2).to_broadcast(shape),
+                op=ALU.mult,
+            )
+            whole = angle_pool.tile(shape, F32, name="whole", tag="whole")
+            nc.gpsimd.tensor_scalar(
+                out=whole[:], in0=angle[:], scalar1=ROUND_MAGIC, scalar2=ROUND_MAGIC,
+                op0=ALU.add, op1=ALU.subtract,
+            )
+            frac = angle_pool.tile(shape, F32, name="frac", tag="frac")
+            nc.gpsimd.tensor_tensor(out=frac[:], in0=angle[:], in1=whole[:], op=ALU.subtract)
+            sin_t = table_pool.tile(shape, F32, name="sin_t", tag="sin_t")
+            nc.scalar.activation(
+                out=sin_t[:, 0:HALF_FT, :], in_=frac[:, 0:HALF_FT, :], func=ACT.Sin,
+                scale=-2.0 * PI,
+            )
+            nc.scalar.activation(
+                out=sin_t[:, HALF_FT:N_FT, :], in_=frac[:, HALF_FT:N_FT, :], func=ACT.Sin,
+                scale=2.0 * PI,
+            )
+            dist = angle_pool.tile(shape, F32, name="dist", tag="dist")
+            nc.scalar.activation(out=dist[:], in_=frac[:], func=ACT.Abs)
+            cos_t = table_pool.tile(shape, F32, name="cos_t", tag="cos_t")
+            nc.scalar.activation(
+                out=cos_t[:], in_=dist[:], func=ACT.Sin, scale=-2.0 * PI, bias=half_pi[:, 0:1]
+            )
+            return cos_t, sin_t
+
+        def quantise_x(xin):
+            grouped = xq_pool.tile([P, TOKENS, 2], F32, name="x_grouped", tag="x_grouped", align_bytes=64)
+            for pair in range(BATCH // 2):
+                xt = xt_psum.tile([P, 2, 2, P], F32, name="xt", tag="xt")
+                for b in range(2):
+                    words = xin[:, 2 * pair + b, :].bitcast(F32)
+                    for u in range(2):
+                        nc.tensor.transpose(
+                            out=xt[:, b, u, :], in_=words[:, u * P : (u + 1) * P], identity=ident[:]
+                        )
+                nc.scalar.copy(
+                    out=grouped[:, 2 * pair * P : (2 * pair + 2) * P, :].rearrange(
+                        "w (b p) u -> w b p u", b=2
+                    ),
+                    in_=xt[:].rearrange("w b u p -> w b p u"),
+                )
+            codes = xq_pool.tile([P, TOKENS], U32, name="x_codes", tag="x_codes", align_bytes=64)
+            scales = xq_pool.tile([P, TOKENS], U8, name="x_scales", tag="x_scales", align_bytes=64)
+            nc.vector.quantize_mx(
+                out=codes[:].bitcast(FP8X4),
+                scales=scales[:],
+                in_=grouped[:].rearrange("w c u -> w (c u)").bitcast(BF16),
+            )
+            return codes, scales
+
+        by_batch = [P, BATCH, P]
+
+        def product(out, bank, bias_col, table):
+            nc.vector.scalar_tensor_tensor(
+                out=out.rearrange("f (b p) -> f b p", b=BATCH),
+                in0=bank[:].rearrange("f (b p) -> f b p", b=BATCH),
+                scalar=bias_col,
+                in1=table.unsqueeze(1).to_broadcast(by_batch),
+                op0=ALU.add,
+                op1=ALU.mult,
+            )
+
+        tables_next = rope_tables(0)
+        x_next = quantise_x(xin_next)
+        weights = (quantise_weight(nc, const, raw_q, "q"), quantise_weight(nc, const, raw_k, "k"))
+        xin_next = load_x(1)
+        for t in range(N_BLOCKS):
+            x_codes, x_scales = x_next
+            cos_t, sin_t = tables_next
+            for z in range(2):
+                w_codes, w_scales = weights[z]
+                stage = stage_pool.tile([P, BATCH, D_OUT], F32, name="stage", tag="stage")
+                for g in range(HALF_FT // 2):
+                    tiles = (2 * g, 2 * g + 1, 2 * g + HALF_FT, 2 * g + 1 + HALF_FT)
+                    banks = {}
+                    for f in tiles:
+                        bank = mx_psum.tile([P, TOKENS], F32, name="bank", tag="bank")
+                        nc.tensor.matmul_mx(
+                            out=bank[:],
+                            lhsT=w_codes[:, f * P : (f + 1) * P].bitcast(FP8X4),
+                            lhsT_scale=w_scales[:, f * P : (f + 1) * P],
+                            rhs=x_codes[:].bitcast(FP8X4),
+                            rhs_scale=x_scales[:],
+                            start=True,
+                            stop=True,
+                        )
+                        banks[f] = bank
+                    own = prod_pool.tile([P, 4, TOKENS], F32, name="own", tag="own")
+                    other = prod_pool.tile([P, 4, TOKENS], F32, name="other", tag="other")
+                    for i, f in enumerate(tiles):
+                        partner = (f + HALF_FT) % N_FT
+                        product(own[:, i, :], banks[f], bias[:, z * N_FT + f : z * N_FT + f + 1], cos_t[:, f, :])
+                        product(
+                            other[:, i, :], banks[partner],
+                            bias[:, z * N_FT + partner : z * N_FT + partner + 1], sin_t[:, f, :],
+                        )
+                    for b in range(BATCH):
+                        sums = sum_psum.tile([P, 4, P], F32, name="sums", tag="sums")
+                        for i in range(4):
+                            nc.tensor.matmul(
+                                out=sums[:, i, :], lhsT=own[:, i, b * P : (b + 1) * P], rhs=ident[:],
+                                is_transpose=True, start=True, stop=False,
+                            )
+                            nc.tensor.matmul(
+                                out=sums[:, i, :], lhsT=other[:, i, b * P : (b + 1) * P], rhs=ident[:],
+                                is_transpose=True, start=False, stop=True,
+                            )
+                        nc.scalar.copy(
+                            out=stage[:, b, :].rearrange("p (h c) -> p h c", h=2)[
+                                :, :, 2 * g * P : (2 * g + 2) * P
+                            ],
+                            in_=sums[:].rearrange("p (h i) c -> p h (i c)", h=2),
+                        )
+                for b in range(BATCH):
+                    nc.sync.dma_start(out=outs[z][b, t * P : (t + 1) * P, :], in_=stage[:, b, :])
+                if z == 0 and t + 1 < N_BLOCKS:
+                    x_next = quantise_x(xin_next)
+                    tables_next = rope_tables(t + 1)
+                    if t + 2 < N_BLOCKS:
+                        xin_next = load_x(t + 2)

@@ -22,7 +22,8 @@ N_BLOCKS = SEQ // P
 TOKENS = BATCH * P
 N_FT = D_OUT // P
 HALF_FT = N_FT // 2
-WORDS = D_IN // 2
+PAIRS_PER_BLOCK = 2 * HALF_FT
+N_PAIRS = N_BLOCKS * PAIRS_PER_BLOCK
 
 FREQ_STEP = ROPE_BASE ** (-2.0 / D_OUT)
 ROUND_MAGIC = 12582912.0
@@ -30,61 +31,46 @@ ROUND_MAGIC = 12582912.0
 FLOPS = 2 * BATCH * SEQ * D_IN * 2 * D_OUT
 
 
-def load_weight(nc, pool, w, label):
-    raw = pool.tile([P, PACK, D_OUT], BF16, name="raw_" + label)
-    for u in range(2):
-        nc.sync.dma_start(
-            out=raw[:, 2 * u : 2 * u + 2, :],
-            in_=w[u * 2 * P : (u + 1) * 2 * P, :].rearrange("(q e) c -> q e c", e=2),
-        )
-    return raw
-
-
-def quantise_weight(nc, pool, raw, label):
-    grouped = pool.tile([P, D_OUT, PACK], BF16, name="grouped_" + label, align_bytes=64)
-    nc.vector.tensor_copy(
-        out=grouped[:].rearrange("p (c i) t -> p c t i", i=4),
-        in_=raw[:].rearrange("p t (c i) -> p c t i", i=4),
-    )
-    codes = pool.tile([P, D_OUT], U32, name="codes_" + label, align_bytes=64)
-    scales = pool.tile([P, D_OUT], U8, name="scales_" + label, align_bytes=64)
-    nc.vector.quantize_mx(
-        out=codes[:].bitcast(FP8X4),
-        scales=scales[:],
-        in_=grouped[:].rearrange("p c t -> p (c t)"),
-    )
-    return codes, scales
-
-
 def tile_ropemultiheadattention_pa_t_kernel(tc, x, Wq, bq, Wk, bk, out_0, out_1):
     nc = tc.nc
     outs = (out_0, out_1)
     with ExitStack() as ctx:
+        ctx.enter_context(tc.manual_schedule())
         const = ctx.enter_context(tc.tile_pool(name="const", bufs=1))
-        xin_pool = ctx.enter_context(tc.tile_pool(name="xin", bufs=3))
         xq_pool = ctx.enter_context(tc.tile_pool(name="xq", bufs=2))
         angle_pool = ctx.enter_context(tc.tile_pool(name="angle", bufs=1))
         table_pool = ctx.enter_context(tc.tile_pool(name="table", bufs=2))
         prod_pool = ctx.enter_context(tc.tile_pool(name="prod", bufs=3))
-        stage_pool = ctx.enter_context(tc.tile_pool(name="stage", bufs=2))
+        stage_pool = ctx.enter_context(tc.tile_pool(name="stage", bufs=3))
         mx_psum = ctx.enter_context(tc.psum_pool(name="mx_psum", bufs=4))
         sum_psum = ctx.enter_context(tc.psum_pool(name="sum_psum", bufs=3))
         xt_psum = ctx.enter_context(tc.psum_pool(name="xt_psum", bufs=1))
 
-        def load_x(t):
-            xin = xin_pool.tile([P, BATCH, D_IN], BF16, name="xin", tag="xin")
-            nc.sync.dma_start(
-                out=xin[:], in_=x[:, t * P : (t + 1) * P, :].rearrange("b p k -> p b k")
-            )
-            return xin
+        xin = const.tile([P, N_BLOCKS, BATCH, D_IN], BF16, name="xin")
 
-        xin_next = load_x(0)
-        raw_q = load_weight(nc, const, Wq, "q")
+        def load_x(t):
+            nc.sync.dma_start(
+                out=xin[:, t, :, :], in_=x[:, t * P : (t + 1) * P, :].rearrange("b p k -> p b k")
+            )
+
+        def load_weight(w, label):
+            raw = const.tile([P, PACK, D_OUT], BF16, name="raw_" + label)
+            for u in range(2):
+                nc.sync.dma_start(
+                    out=raw[:, 2 * u : 2 * u + 2, :],
+                    in_=w[u * 2 * P : (u + 1) * 2 * P, :].rearrange("(q e) c -> q e c", e=2),
+                )
+            return raw
+
         bias_rows = const.tile([P, P], BF16, name="bias_rows")
         nc.vector.memset(bias_rows[:], 0.0)
+        load_x(0)
+        raw = [load_weight(Wq, "q")]
         nc.sync.dma_start(out=bias_rows[0:N_FT, :], in_=bq.rearrange("(r c) -> r c", c=P))
         nc.sync.dma_start(out=bias_rows[N_FT : 2 * N_FT, :], in_=bk.rearrange("(r c) -> r c", c=P))
-        raw_k = load_weight(nc, const, Wk, "k")
+        raw.append(load_weight(Wk, "k"))
+        for t in range(1, N_BLOCKS):
+            load_x(t)
 
         ident = const.tile([P, P], F32, name="ident")
         masks.make_identity(nc, ident[:])
@@ -105,16 +91,17 @@ def tile_ropemultiheadattention_pa_t_kernel(tc, x, Wq, bq, Wk, bk, out_0, out_1)
             )
             w *= 2
 
-        bias_rows_f32 = const.tile([P, P], F32, name="bias_rows_f32")
-        nc.vector.tensor_copy(out=bias_rows_f32[:], in_=bias_rows[:])
-        setup = xt_psum.tile([P, 2, P], F32, name="setup", tag="xt")
-        nc.tensor.transpose(out=setup[:, 0, :], in_=bias_rows_f32[:], identity=ident[:])
-        nc.tensor.transpose(out=setup[:, 1, :], in_=step_row[:], identity=ident[:])
-        bias = const.tile([P, 2 * N_FT], F32, name="bias")
-        nc.vector.tensor_copy(out=bias[:], in_=setup[:, 0, 0 : 2 * N_FT])
+        half_pi = const.tile([P, 1], F32, name="half_pi")
+        nc.vector.memset(half_pi[:], 1.0)
+        nc.vector.tensor_scalar_mul(out=half_pi[:], in0=half_pi[:], scalar1=PI / 2.0)
+        warm = const.tile([P, 1], F32, name="warm")
+        nc.scalar.activation(out=warm[:], in_=half_pi[:], func=ACT.Sin)
+
+        step_col = sum_psum.tile([P, P], F32, name="step_col", tag="sums")
+        nc.tensor.transpose(out=step_col[:], in_=step_row[:], identity=ident[:])
         turns = const.tile([P, N_FT], F32, name="turns")
         nc.vector.tensor_scalar_mul(
-            out=turns[:, 0:1], in0=setup[:, 1, 0:1], scalar1=1.0 / (2.0 * PI)
+            out=turns[:, 0:1], in0=step_col[:, 0:1], scalar1=1.0 / (2.0 * PI)
         )
         w = 1
         while w < N_FT:
@@ -122,135 +109,210 @@ def tile_ropemultiheadattention_pa_t_kernel(tc, x, Wq, bq, Wk, bk, out_0, out_1)
                 out=turns[:, w : 2 * w], in0=turns[:, 0:w], scalar1=FREQ_STEP ** (w * P // 2)
             )
             w *= 2
-        half_pi = const.tile([P, 1], F32, name="half_pi")
-        nc.vector.memset(half_pi[:], 1.0)
-        nc.vector.tensor_scalar_mul(out=half_pi[:], in0=half_pi[:], scalar1=PI / 2.0)
 
-        def rope_tables(t):
-            shape = [P, N_FT, P]
-            angle = angle_pool.tile(shape, F32, name="angle", tag="angle")
-            nc.gpsimd.tensor_tensor(
+        w_grouped = [const.tile([P, HALF_FT, 2, P, PACK], BF16, name="w_grouped%d" % z, align_bytes=64) for z in range(2)]
+        w_codes = [const.tile([P, HALF_FT, 2, P], U32, name="w_codes%d" % z, align_bytes=64) for z in range(2)]
+        w_scales = [const.tile([P, HALF_FT, 2, P], U8, name="w_scales%d" % z, align_bytes=64) for z in range(2)]
+
+        def group_weight(z, f):
+            src = raw[z][:].rearrange("p t (h f c) -> p f h c t", h=2, f=HALF_FT)[:, f, :, :, :]
+            if z == 0:
+                nc.vector.tensor_copy(out=w_grouped[z][:, f, :, :, :], in_=src)
+            else:
+                nc.scalar.copy(out=w_grouped[z][:, f, :, :, :], in_=src)
+
+        def quantise_weight(z, f):
+            nc.vector.quantize_mx(
+                out=w_codes[z][:, f, :, :].rearrange("p h c -> p (h c)").bitcast(FP8X4),
+                scales=w_scales[z][:, f, :, :].rearrange("p h c -> p (h c)"),
+                in_=w_grouped[z][:, f, :, :, :].rearrange("p h c t -> p (h c t)"),
+            )
+
+        table_shape = [P, N_FT, P]
+        frac_of, dist_of, tables_of, x_grouped_of, x_quantised_of = {}, {}, {}, {}, {}
+
+        def angles(t, engine):
+            angle = angle_pool.tile(table_shape, F32, name="angle", tag="angle")
+            engine.tensor_tensor(
                 out=angle[:],
-                in0=pos[:, t * P : (t + 1) * P].unsqueeze(1).to_broadcast(shape),
-                in1=turns[:].unsqueeze(2).to_broadcast(shape),
+                in0=pos[:, t * P : (t + 1) * P].unsqueeze(1).to_broadcast(table_shape),
+                in1=turns[:].unsqueeze(2).to_broadcast(table_shape),
                 op=ALU.mult,
             )
-            whole = angle_pool.tile(shape, F32, name="whole", tag="whole")
-            nc.gpsimd.tensor_scalar(
+            whole = angle_pool.tile(table_shape, F32, name="whole", tag="whole")
+            engine.tensor_scalar(
                 out=whole[:], in0=angle[:], scalar1=ROUND_MAGIC, scalar2=ROUND_MAGIC,
                 op0=ALU.add, op1=ALU.subtract,
             )
-            frac = angle_pool.tile(shape, F32, name="frac", tag="frac")
-            nc.gpsimd.tensor_tensor(out=frac[:], in0=angle[:], in1=whole[:], op=ALU.subtract)
-            sin_t = table_pool.tile(shape, F32, name="sin_t", tag="sin_t")
-            nc.scalar.activation(
-                out=sin_t[:, 0:HALF_FT, :], in_=frac[:, 0:HALF_FT, :], func=ACT.Sin,
-                scale=-2.0 * PI,
-            )
-            nc.scalar.activation(
-                out=sin_t[:, HALF_FT:N_FT, :], in_=frac[:, HALF_FT:N_FT, :], func=ACT.Sin,
-                scale=2.0 * PI,
-            )
-            dist = angle_pool.tile(shape, F32, name="dist", tag="dist")
-            nc.scalar.activation(out=dist[:], in_=frac[:], func=ACT.Abs)
-            cos_t = table_pool.tile(shape, F32, name="cos_t", tag="cos_t")
-            nc.scalar.activation(
-                out=cos_t[:], in_=dist[:], func=ACT.Sin, scale=-2.0 * PI, bias=half_pi[:, 0:1]
-            )
-            return cos_t, sin_t
+            frac = angle_pool.tile(table_shape, F32, name="frac", tag="frac")
+            engine.tensor_tensor(out=frac[:], in0=angle[:], in1=whole[:], op=ALU.subtract)
+            frac_of[t] = frac
+            cos_t = table_pool.tile(table_shape, F32, name="cos_t", tag="cos_t")
+            sin_t = table_pool.tile(table_shape, F32, name="sin_t", tag="sin_t")
+            tables_of[t] = (cos_t, sin_t)
 
-        def quantise_x(xin):
-            grouped = xq_pool.tile([P, TOKENS, 2], F32, name="x_grouped", tag="x_grouped", align_bytes=64)
-            for pair in range(BATCH // 2):
-                xt = xt_psum.tile([P, 2, 2, P], F32, name="xt", tag="xt")
-                for b in range(2):
-                    words = xin[:, 2 * pair + b, :].bitcast(F32)
-                    for u in range(2):
-                        nc.tensor.transpose(
-                            out=xt[:, b, u, :], in_=words[:, u * P : (u + 1) * P], identity=ident[:]
-                        )
-                nc.scalar.copy(
-                    out=grouped[:, 2 * pair * P : (2 * pair + 2) * P, :].rearrange(
-                        "w (b p) u -> w b p u", b=2
-                    ),
-                    in_=xt[:].rearrange("w b u p -> w b p u"),
-                )
+        def sine(t, half):
+            tiles = slice(half * HALF_FT, (half + 1) * HALF_FT)
+            nc.scalar.activation(
+                out=tables_of[t][1][:, tiles, :], in_=frac_of[t][:, tiles, :], func=ACT.Sin,
+                scale=(2 * half - 1) * 2.0 * PI,
+            )
+
+        def distance(t):
+            dist = angle_pool.tile(table_shape, F32, name="dist", tag="dist")
+            nc.scalar.activation(out=dist[:], in_=frac_of[t][:], func=ACT.Abs)
+            dist_of[t] = dist
+
+        def cosine(t):
+            nc.scalar.activation(
+                out=tables_of[t][0][:], in_=dist_of[t][:], func=ACT.Sin, scale=-2.0 * PI,
+                bias=half_pi[:, 0:1],
+            )
+
+        def turn_x(t, first):
+            if first == 0:
+                x_grouped_of[t] = xq_pool.tile([P, TOKENS, 2], F32, name="x_grouped", tag="x_grouped", align_bytes=64)
+            xt = xt_psum.tile([P, 2, 2, P], F32, name="xt", tag="xt")
+            for b in range(2):
+                words = xin[:, t, first + b, :].bitcast(F32)
+                for u in range(2):
+                    nc.tensor.transpose(out=xt[:, b, u, :], in_=words[:, u * P : (u + 1) * P], identity=ident[:])
+            nc.scalar.copy(
+                out=x_grouped_of[t][:, first * P : (first + 2) * P, :].rearrange("w (b p) u -> w b p u", b=2),
+                in_=xt[:].rearrange("w b u p -> w b p u"),
+            )
+
+        def quantise_x(t):
             codes = xq_pool.tile([P, TOKENS], U32, name="x_codes", tag="x_codes", align_bytes=64)
             scales = xq_pool.tile([P, TOKENS], U8, name="x_scales", tag="x_scales", align_bytes=64)
             nc.vector.quantize_mx(
                 out=codes[:].bitcast(FP8X4),
                 scales=scales[:],
-                in_=grouped[:].rearrange("w c u -> w (c u)").bitcast(BF16),
+                in_=x_grouped_of[t][:].rearrange("w c u -> w (c u)").bitcast(BF16),
             )
-            return codes, scales
+            x_quantised_of[t] = (codes, scales)
 
-        by_batch = [P, BATCH, P]
+        def prepare(t, part, engine):
+            if part == 0:
+                angles(t, engine)
+                turn_x(t, 0)
+            elif part == 1:
+                turn_x(t, 2)
+            elif part == 2:
+                quantise_x(t)
+            elif part == 3:
+                sine(t, 0)
+            elif part == 4:
+                sine(t, 1)
+            elif part == 5:
+                distance(t)
+            elif part == 6:
+                cosine(t)
+
+        banks_of, products_of, stage_of = {}, {}, {}
+        by_sequence = [P, BATCH, P]
+
+        def where(k):
+            t, rest = divmod(k, PAIRS_PER_BLOCK)
+            z, f = divmod(rest, HALF_FT)
+            return t, z, f
+
+        def project(k):
+            t, z, f = where(k)
+            x_codes, x_scales = x_quantised_of[t]
+            banks = []
+            for h in range(2):
+                bank = mx_psum.tile([P, TOKENS], F32, name="bank", tag="bank")
+                nc.tensor.matmul_mx(
+                    out=bank[:],
+                    lhsT=w_codes[z][:, f, h, :].bitcast(FP8X4),
+                    lhsT_scale=w_scales[z][:, f, h, :],
+                    rhs=x_codes[:].bitcast(FP8X4),
+                    rhs_scale=x_scales[:],
+                    start=True,
+                    stop=True,
+                )
+                banks.append(bank)
+            banks_of[k] = banks
 
         def product(out, bank, bias_col, table):
             nc.vector.scalar_tensor_tensor(
                 out=out.rearrange("f (b p) -> f b p", b=BATCH),
                 in0=bank[:].rearrange("f (b p) -> f b p", b=BATCH),
                 scalar=bias_col,
-                in1=table.unsqueeze(1).to_broadcast(by_batch),
+                in1=table.unsqueeze(1).to_broadcast(by_sequence),
                 op0=ALU.add,
                 op1=ALU.mult,
             )
 
-        tables_next = rope_tables(0)
-        x_next = quantise_x(xin_next)
-        weights = (quantise_weight(nc, const, raw_q, "q"), quantise_weight(nc, const, raw_k, "k"))
-        xin_next = load_x(1)
-        for t in range(N_BLOCKS):
-            x_codes, x_scales = x_next
-            cos_t, sin_t = tables_next
-            for z in range(2):
-                w_codes, w_scales = weights[z]
-                stage = stage_pool.tile([P, BATCH, D_OUT], F32, name="stage", tag="stage")
-                for g in range(HALF_FT // 2):
-                    tiles = (2 * g, 2 * g + 1, 2 * g + HALF_FT, 2 * g + 1 + HALF_FT)
-                    banks = {}
-                    for f in tiles:
-                        bank = mx_psum.tile([P, TOKENS], F32, name="bank", tag="bank")
-                        nc.tensor.matmul_mx(
-                            out=bank[:],
-                            lhsT=w_codes[:, f * P : (f + 1) * P].bitcast(FP8X4),
-                            lhsT_scale=w_scales[:, f * P : (f + 1) * P],
-                            rhs=x_codes[:].bitcast(FP8X4),
-                            rhs_scale=x_scales[:],
-                            start=True,
-                            stop=True,
+        def rotate(k):
+            t, z, f = where(k)
+            cos_t, sin_t = tables_of[t]
+            own = prod_pool.tile([P, 2, TOKENS], F32, name="own", tag="own")
+            other = prod_pool.tile([P, 2, TOKENS], F32, name="other", tag="other")
+            for h in range(2):
+                tile_here = f + h * HALF_FT
+                tile_there = f + (1 - h) * HALF_FT
+                bias_col = bias[:, z * N_FT + tile_here : z * N_FT + tile_here + 1]
+                product(own[:, h, :], banks_of[k][h], bias_col, cos_t[:, tile_here, :])
+                product(other[:, 1 - h, :], banks_of[k][h], bias_col, sin_t[:, tile_there, :])
+            products_of[k] = (own, other)
+
+        def sum_and_turn(k):
+            t, z, f = where(k)
+            own, other = products_of[k]
+            if f == 0:
+                stage_of[(t, z)] = stage_pool.tile([P, BATCH, D_OUT], F32, name="stage", tag="stage")
+            stage = stage_of[(t, z)]
+            for first in range(0, BATCH, 2):
+                sums = sum_psum.tile([P, 2, 2, P], F32, name="sums", tag="sums")
+                for b in range(2):
+                    tokens = slice((first + b) * P, (first + b + 1) * P)
+                    for h in range(2):
+                        nc.tensor.matmul(
+                            out=sums[:, b, h, :], lhsT=own[:, h, tokens], rhs=ident[:],
+                            is_transpose=True, start=True, stop=False,
                         )
-                        banks[f] = bank
-                    own = prod_pool.tile([P, 4, TOKENS], F32, name="own", tag="own")
-                    other = prod_pool.tile([P, 4, TOKENS], F32, name="other", tag="other")
-                    for i, f in enumerate(tiles):
-                        partner = (f + HALF_FT) % N_FT
-                        product(own[:, i, :], banks[f], bias[:, z * N_FT + f : z * N_FT + f + 1], cos_t[:, f, :])
-                        product(
-                            other[:, i, :], banks[partner],
-                            bias[:, z * N_FT + partner : z * N_FT + partner + 1], sin_t[:, f, :],
+                        nc.tensor.matmul(
+                            out=sums[:, b, h, :], lhsT=other[:, h, tokens], rhs=ident[:],
+                            is_transpose=True, start=False, stop=True,
                         )
-                    for b in range(BATCH):
-                        sums = sum_psum.tile([P, 4, P], F32, name="sums", tag="sums")
-                        for i in range(4):
-                            nc.tensor.matmul(
-                                out=sums[:, i, :], lhsT=own[:, i, b * P : (b + 1) * P], rhs=ident[:],
-                                is_transpose=True, start=True, stop=False,
-                            )
-                            nc.tensor.matmul(
-                                out=sums[:, i, :], lhsT=other[:, i, b * P : (b + 1) * P], rhs=ident[:],
-                                is_transpose=True, start=False, stop=True,
-                            )
-                        nc.scalar.copy(
-                            out=stage[:, b, :].rearrange("p (h c) -> p h c", h=2)[
-                                :, :, 2 * g * P : (2 * g + 2) * P
-                            ],
-                            in_=sums[:].rearrange("p (h i) c -> p h (i c)", h=2),
-                        )
+                nc.scalar.copy(
+                    out=stage[:, first : first + 2, :].rearrange("p b (h c) -> p b h c", h=2)[
+                        :, :, :, f * P : (f + 1) * P
+                    ],
+                    in_=sums[:],
+                )
+            if f == HALF_FT - 1:
                 for b in range(BATCH):
                     nc.sync.dma_start(out=outs[z][b, t * P : (t + 1) * P, :], in_=stage[:, b, :])
-                if z == 0 and t + 1 < N_BLOCKS:
-                    x_next = quantise_x(xin_next)
-                    tables_next = rope_tables(t + 1)
-                    if t + 2 < N_BLOCKS:
-                        xin_next = load_x(t + 2)
+
+        for part in range(PAIRS_PER_BLOCK):
+            prepare(0, part, nc.vector)
+            if part == 1:
+                group_weight(0, 0)
+        quantise_weight(0, 0)
+        project(0)
+        bias_rows_f32 = const.tile([P, P], F32, name="bias_rows_f32")
+        nc.vector.tensor_copy(out=bias_rows_f32[:], in_=bias_rows[:])
+        bias_cols = sum_psum.tile([P, P], F32, name="bias_cols", tag="sums")
+        nc.tensor.transpose(out=bias_cols[:], in_=bias_rows_f32[:], identity=ident[:])
+        bias = const.tile([P, 2 * N_FT], F32, name="bias")
+        nc.vector.tensor_copy(out=bias[:], in_=bias_cols[:, 0 : 2 * N_FT])
+        group_weight(0, 1)
+        quantise_weight(0, 1)
+
+        for k in range(N_PAIRS + 1):
+            if k + 1 < N_PAIRS:
+                project(k + 1)
+            if k < N_PAIRS:
+                rotate(k)
+            if k + 2 < PAIRS_PER_BLOCK:
+                z, f = divmod(k + 2, HALF_FT)
+                group_weight(z, f)
+                quantise_weight(z, f)
+            if k >= 1:
+                sum_and_turn(k - 1)
+            t, part = divmod(k, PAIRS_PER_BLOCK)
+            if t + 1 < N_BLOCKS:
+                prepare(t + 1, part, nc.gpsimd)

@@ -24,6 +24,7 @@ N_FT = D_OUT // P
 HALF_FT = N_FT // 2
 PAIRS_PER_BLOCK = 2 * HALF_FT
 N_PAIRS = N_BLOCKS * PAIRS_PER_BLOCK
+ANGLE_PARTS = 6
 
 FREQ_STEP = ROPE_BASE ** (-2.0 / D_OUT)
 ROUND_MAGIC = 12582912.0
@@ -39,8 +40,9 @@ def tile_ropemultiheadattention_pa_t_kernel(tc, x, Wq, bq, Wk, bk, out_0, out_1)
         const = ctx.enter_context(tc.tile_pool(name="const", bufs=1))
         xq_pool = ctx.enter_context(tc.tile_pool(name="xq", bufs=2))
         angle_pool = ctx.enter_context(tc.tile_pool(name="angle", bufs=1))
+        frac_pool = ctx.enter_context(tc.tile_pool(name="frac", bufs=2))
         table_pool = ctx.enter_context(tc.tile_pool(name="table", bufs=2))
-        prod_pool = ctx.enter_context(tc.tile_pool(name="prod", bufs=3))
+        prod_pool = ctx.enter_context(tc.tile_pool(name="prod", bufs=4))
         stage_pool = ctx.enter_context(tc.tile_pool(name="stage", bufs=3))
         mx_psum = ctx.enter_context(tc.psum_pool(name="mx_psum", bufs=4))
         sum_psum = ctx.enter_context(tc.psum_pool(name="sum_psum", bufs=3))
@@ -129,30 +131,39 @@ def tile_ropemultiheadattention_pa_t_kernel(tc, x, Wq, bq, Wk, bk, out_0, out_1)
             )
 
         table_shape = [P, N_FT, P]
-        frac_of, dist_of, tables_of, x_grouped_of, x_quantised_of = {}, {}, {}, {}, {}
+        angle_of, whole_of, frac_of, dist_of, tables_of = {}, {}, {}, {}, {}
+        x_grouped_of, x_quantised_of = {}, {}
 
-        def angles(t, engine):
-            angle = angle_pool.tile(table_shape, F32, name="angle", tag="angle")
-            engine.tensor_tensor(
-                out=angle[:],
-                in0=pos[:, t * P : (t + 1) * P].unsqueeze(1).to_broadcast(table_shape),
-                in1=turns[:].unsqueeze(2).to_broadcast(table_shape),
-                op=ALU.mult,
-            )
-            whole = angle_pool.tile(table_shape, F32, name="whole", tag="whole")
-            engine.tensor_scalar(
-                out=whole[:], in0=angle[:], scalar1=ROUND_MAGIC, scalar2=ROUND_MAGIC,
-                op0=ALU.add, op1=ALU.subtract,
-            )
-            frac = angle_pool.tile(table_shape, F32, name="frac", tag="frac")
-            engine.tensor_tensor(out=frac[:], in0=angle[:], in1=whole[:], op=ALU.subtract)
-            frac_of[t] = frac
-            cos_t = table_pool.tile(table_shape, F32, name="cos_t", tag="cos_t")
-            sin_t = table_pool.tile(table_shape, F32, name="sin_t", tag="sin_t")
-            tables_of[t] = (cos_t, sin_t)
+        def angles(t, part, engine):
+            half, instruction = divmod(part, 3)
+            tiles = slice(half * HALF_FT, (half + 1) * HALF_FT)
+            shape = [P, HALF_FT, P]
+            if part == 0:
+                angle_of[t] = angle_pool.tile(table_shape, F32, name="angle", tag="angle")
+                whole_of[t] = angle_pool.tile(table_shape, F32, name="whole", tag="whole")
+                frac_of[t] = frac_pool.tile(table_shape, F32, name="frac", tag="frac")
+            angle, whole, frac = angle_of[t][:, tiles, :], whole_of[t][:, tiles, :], frac_of[t][:, tiles, :]
+            if instruction == 0:
+                engine.tensor_tensor(
+                    out=angle,
+                    in0=pos[:, t * P : (t + 1) * P].unsqueeze(1).to_broadcast(shape),
+                    in1=turns[:, tiles].unsqueeze(2).to_broadcast(shape),
+                    op=ALU.mult,
+                )
+            elif instruction == 1:
+                engine.tensor_scalar(
+                    out=whole, in0=angle, scalar1=ROUND_MAGIC, scalar2=ROUND_MAGIC,
+                    op0=ALU.add, op1=ALU.subtract,
+                )
+            else:
+                engine.tensor_tensor(out=frac, in0=angle, in1=whole, op=ALU.subtract)
 
         def sine(t, half):
             tiles = slice(half * HALF_FT, (half + 1) * HALF_FT)
+            if half == 0:
+                cos_t = table_pool.tile(table_shape, F32, name="cos_t", tag="cos_t")
+                sin_t = table_pool.tile(table_shape, F32, name="sin_t", tag="sin_t")
+                tables_of[t] = (cos_t, sin_t)
             nc.scalar.activation(
                 out=tables_of[t][1][:, tiles, :], in_=frac_of[t][:, tiles, :], func=ACT.Sin,
                 scale=(2 * half - 1) * 2.0 * PI,
@@ -192,21 +203,19 @@ def tile_ropemultiheadattention_pa_t_kernel(tc, x, Wq, bq, Wk, bk, out_0, out_1)
             )
             x_quantised_of[t] = (codes, scales)
 
-        def prepare(t, part, engine):
+        def prepare(t, part):
             if part == 0:
-                angles(t, engine)
                 turn_x(t, 0)
             elif part == 1:
                 turn_x(t, 2)
             elif part == 2:
                 quantise_x(t)
-            elif part == 3:
                 sine(t, 0)
-            elif part == 4:
+            elif part == 3:
                 sine(t, 1)
-            elif part == 5:
+            elif part == 4:
                 distance(t)
-            elif part == 6:
+            elif part == 5:
                 cosine(t)
 
         banks_of, products_of, stage_of = {}, {}, {}
@@ -258,6 +267,10 @@ def tile_ropemultiheadattention_pa_t_kernel(tc, x, Wq, bq, Wk, bk, out_0, out_1)
                 product(other[:, 1 - h, :], banks_of[k][h], bias_col, sin_t[:, tile_there, :])
             products_of[k] = (own, other)
 
+        def add_upper(k):
+            own, other = products_of[k]
+            nc.gpsimd.tensor_tensor(out=own[:, 1, :], in0=own[:, 1, :], in1=other[:, 1, :], op=ALU.add)
+
         def sum_and_turn(k):
             t, z, f = where(k)
             own, other = products_of[k]
@@ -268,15 +281,15 @@ def tile_ropemultiheadattention_pa_t_kernel(tc, x, Wq, bq, Wk, bk, out_0, out_1)
                 sums = sum_psum.tile([P, 2, 2, P], F32, name="sums", tag="sums")
                 for b in range(2):
                     tokens = slice((first + b) * P, (first + b + 1) * P)
-                    for h in range(2):
-                        nc.tensor.matmul(
-                            out=sums[:, b, h, :], lhsT=own[:, h, tokens], rhs=ident[:],
-                            is_transpose=True, start=True, stop=False,
-                        )
-                        nc.tensor.matmul(
-                            out=sums[:, b, h, :], lhsT=other[:, h, tokens], rhs=ident[:],
-                            is_transpose=True, start=False, stop=True,
-                        )
+                    nc.tensor.matmul(
+                        out=sums[:, b, 0, :], lhsT=own[:, 0, tokens], rhs=ident[:],
+                        is_transpose=True, start=True, stop=False,
+                    )
+                    nc.tensor.matmul(
+                        out=sums[:, b, 0, :], lhsT=other[:, 0, tokens], rhs=ident[:],
+                        is_transpose=True, start=False, stop=True,
+                    )
+                    nc.tensor.transpose(out=sums[:, b, 1, :], in_=own[:, 1, tokens], identity=ident[:])
                 nc.scalar.copy(
                     out=stage[:, first : first + 2, :].rearrange("p b (h c) -> p b h c", h=2)[
                         :, :, :, f * P : (f + 1) * P
@@ -287,8 +300,12 @@ def tile_ropemultiheadattention_pa_t_kernel(tc, x, Wq, bq, Wk, bk, out_0, out_1)
                 for b in range(BATCH):
                     nc.sync.dma_start(out=outs[z][b, t * P : (t + 1) * P, :], in_=stage[:, b, :])
 
+        for part in range(ANGLE_PARTS):
+            angles(0, part, nc.vector)
+        for part in range(ANGLE_PARTS):
+            angles(1, part, nc.gpsimd)
         for part in range(PAIRS_PER_BLOCK):
-            prepare(0, part, nc.vector)
+            prepare(0, part)
             if part == 1:
                 group_weight(0, 0)
         quantise_weight(0, 0)
@@ -302,7 +319,7 @@ def tile_ropemultiheadattention_pa_t_kernel(tc, x, Wq, bq, Wk, bk, out_0, out_1)
         group_weight(0, 1)
         quantise_weight(0, 1)
 
-        for k in range(N_PAIRS + 1):
+        for k in range(N_PAIRS + 2):
             if k + 1 < N_PAIRS:
                 project(k + 1)
             if k < N_PAIRS:
@@ -311,8 +328,12 @@ def tile_ropemultiheadattention_pa_t_kernel(tc, x, Wq, bq, Wk, bk, out_0, out_1)
                 z, f = divmod(k + 2, HALF_FT)
                 group_weight(z, f)
                 quantise_weight(z, f)
-            if k >= 1:
-                sum_and_turn(k - 1)
+            if 1 <= k <= N_PAIRS:
+                add_upper(k - 1)
+            if k >= 2:
+                sum_and_turn(k - 2)
             t, part = divmod(k, PAIRS_PER_BLOCK)
             if t + 1 < N_BLOCKS:
-                prepare(t + 1, part, nc.gpsimd)
+                prepare(t + 1, part)
+            if t + 2 < N_BLOCKS and part < ANGLE_PARTS:
+                angles(t + 2, part, nc.gpsimd)

@@ -24,7 +24,7 @@ N_FT = D_OUT // P
 HALF_FT = N_FT // 2
 PAIRS_PER_BLOCK = 2 * HALF_FT
 N_PAIRS = N_BLOCKS * PAIRS_PER_BLOCK
-ANGLE_PARTS = 6
+N_TRIG = 2 * N_FT
 
 FREQ_STEP = ROPE_BASE ** (-2.0 / D_OUT)
 ROUND_MAGIC = 12582912.0
@@ -39,10 +39,9 @@ def tile_ropemultiheadattention_pa_t_kernel(tc, x, Wq, bq, Wk, bk, out_0, out_1)
         ctx.enter_context(tc.manual_schedule())
         const = ctx.enter_context(tc.tile_pool(name="const", bufs=1))
         xq_pool = ctx.enter_context(tc.tile_pool(name="xq", bufs=2))
-        angle_pool = ctx.enter_context(tc.tile_pool(name="angle", bufs=1))
-        frac_pool = ctx.enter_context(tc.tile_pool(name="frac", bufs=2))
-        table_pool = ctx.enter_context(tc.tile_pool(name="table", bufs=2))
-        prod_pool = ctx.enter_context(tc.tile_pool(name="prod", bufs=4))
+        fold_pool = ctx.enter_context(tc.tile_pool(name="fold", bufs=1))
+        trig_pool = ctx.enter_context(tc.tile_pool(name="trig", bufs=2))
+        prod_pool = ctx.enter_context(tc.tile_pool(name="prod", bufs=3))
         stage_pool = ctx.enter_context(tc.tile_pool(name="stage", bufs=3))
         mx_psum = ctx.enter_context(tc.psum_pool(name="mx_psum", bufs=4))
         sum_psum = ctx.enter_context(tc.psum_pool(name="sum_psum", bufs=3))
@@ -77,10 +76,10 @@ def tile_ropemultiheadattention_pa_t_kernel(tc, x, Wq, bq, Wk, bk, out_0, out_1)
         ident = const.tile([P, P], F32, name="ident")
         masks.make_identity(nc, ident[:])
 
-        pos = const.tile([P, SEQ], F32, name="pos")
+        pos = const.tile([P, P], F32, name="pos")
         nc.vector.memset(pos[:, 0:1], 0.0)
         w = 1
-        while w < SEQ:
+        while w < P:
             nc.vector.tensor_scalar_add(out=pos[:, w : 2 * w], in0=pos[:, 0:w], scalar1=float(w))
             w *= 2
 
@@ -93,9 +92,12 @@ def tile_ropemultiheadattention_pa_t_kernel(tc, x, Wq, bq, Wk, bk, out_0, out_1)
             )
             w *= 2
 
+        minus_half = const.tile([P, 1], F32, name="minus_half")
+        nc.vector.memset(minus_half[:], -0.5)
         half_pi = const.tile([P, 1], F32, name="half_pi")
-        nc.vector.memset(half_pi[:], 1.0)
-        nc.vector.tensor_scalar_mul(out=half_pi[:], in0=half_pi[:], scalar1=PI / 2.0)
+        nc.vector.tensor_scalar_mul(out=half_pi[:], in0=minus_half[:], scalar1=-PI)
+        minus_half_pi = const.tile([P, 1], F32, name="minus_half_pi")
+        nc.vector.tensor_scalar_mul(out=minus_half_pi[:], in0=minus_half[:], scalar1=PI)
         warm = const.tile([P, 1], F32, name="warm")
         nc.scalar.activation(out=warm[:], in_=half_pi[:], func=ACT.Sin)
 
@@ -112,72 +114,88 @@ def tile_ropemultiheadattention_pa_t_kernel(tc, x, Wq, bq, Wk, bk, out_0, out_1)
             )
             w *= 2
 
-        w_grouped = [const.tile([P, HALF_FT, 2, P, PACK], BF16, name="w_grouped%d" % z, align_bytes=64) for z in range(2)]
-        w_codes = [const.tile([P, HALF_FT, 2, P], U32, name="w_codes%d" % z, align_bytes=64) for z in range(2)]
-        w_scales = [const.tile([P, HALF_FT, 2, P], U8, name="w_scales%d" % z, align_bytes=64) for z in range(2)]
-
-        def group_weight(z, f):
-            src = raw[z][:].rearrange("p t (h f c) -> p f h c t", h=2, f=HALF_FT)[:, f, :, :, :]
-            if z == 0:
-                nc.vector.tensor_copy(out=w_grouped[z][:, f, :, :, :], in_=src)
-            else:
-                nc.scalar.copy(out=w_grouped[z][:, f, :, :, :], in_=src)
-
-        def quantise_weight(z, f):
-            nc.vector.quantize_mx(
-                out=w_codes[z][:, f, :, :].rearrange("p h c -> p (h c)").bitcast(FP8X4),
-                scales=w_scales[z][:, f, :, :].rearrange("p h c -> p (h c)"),
-                in_=w_grouped[z][:, f, :, :, :].rearrange("p h c t -> p (h c t)"),
+        def nearest_whole_removed(out, value, scratch):
+            nc.vector.tensor_scalar(
+                out=scratch, in0=value, scalar1=ROUND_MAGIC, scalar2=ROUND_MAGIC,
+                op0=ALU.add, op1=ALU.subtract,
             )
+            nc.vector.tensor_tensor(out=out, in0=value, in1=scratch, op=ALU.subtract)
 
         table_shape = [P, N_FT, P]
-        angle_of, whole_of, frac_of, dist_of, tables_of = {}, {}, {}, {}, {}
-        x_grouped_of, x_quantised_of = {}, {}
+        angle0 = const.tile(table_shape, F32, name="angle0")
+        nc.vector.tensor_tensor(
+            out=angle0[:],
+            in0=pos[:].unsqueeze(1).to_broadcast(table_shape),
+            in1=turns[:].unsqueeze(2).to_broadcast(table_shape),
+            op=ALU.mult,
+        )
+        whole0 = const.tile(table_shape, F32, name="whole0")
+        frac0 = const.tile(table_shape, F32, name="frac0")
+        nearest_whole_removed(frac0[:], angle0[:], whole0[:])
 
-        def angles(t, part, engine):
-            half, instruction = divmod(part, 3)
-            tiles = slice(half * HALF_FT, (half + 1) * HALF_FT)
-            shape = [P, HALF_FT, P]
-            if part == 0:
-                angle_of[t] = angle_pool.tile(table_shape, F32, name="angle", tag="angle")
-                whole_of[t] = angle_pool.tile(table_shape, F32, name="whole", tag="whole")
-                frac_of[t] = frac_pool.tile(table_shape, F32, name="frac", tag="frac")
-            angle, whole, frac = angle_of[t][:, tiles, :], whole_of[t][:, tiles, :], frac_of[t][:, tiles, :]
-            if instruction == 0:
-                engine.tensor_tensor(
-                    out=angle,
-                    in0=pos[:, t * P : (t + 1) * P].unsqueeze(1).to_broadcast(shape),
-                    in1=turns[:, tiles].unsqueeze(2).to_broadcast(shape),
-                    op=ALU.mult,
-                )
-            elif instruction == 1:
-                engine.tensor_scalar(
-                    out=whole, in0=angle, scalar1=ROUND_MAGIC, scalar2=ROUND_MAGIC,
-                    op0=ALU.add, op1=ALU.subtract,
-                )
-            else:
-                engine.tensor_tensor(out=frac, in0=angle, in1=whole, op=ALU.subtract)
+        block_shape = [P, N_BLOCKS, N_FT]
+        block_turns = const.tile([P, N_FT], F32, name="block_turns")
+        nc.vector.tensor_scalar_mul(out=block_turns[:], in0=turns[:], scalar1=float(P))
+        block_angle = const.tile(block_shape, F32, name="block_angle")
+        nc.vector.tensor_tensor(
+            out=block_angle[:],
+            in0=pos[:, 0:N_BLOCKS].unsqueeze(2).to_broadcast(block_shape),
+            in1=block_turns[:].unsqueeze(1).to_broadcast(block_shape),
+            op=ALU.mult,
+        )
+        block_whole = const.tile(block_shape, F32, name="block_whole")
+        shifts = const.tile([P, N_BLOCKS, N_TRIG], F32, name="shifts")
+        nearest_whole_removed(shifts[:, :, N_FT:N_TRIG], block_angle[:], block_whole[:])
+        nc.vector.tensor_scalar_add(out=shifts[:, :, 0:N_FT], in0=shifts[:, :, N_FT:N_TRIG], scalar1=-0.25)
 
-        def sine(t, half):
-            tiles = slice(half * HALF_FT, (half + 1) * HALF_FT)
-            if half == 0:
-                cos_t = table_pool.tile(table_shape, F32, name="cos_t", tag="cos_t")
-                sin_t = table_pool.tile(table_shape, F32, name="sin_t", tag="sin_t")
-                tables_of[t] = (cos_t, sin_t)
+        def group_weight(z):
+            grouped = const.tile([P, D_OUT, PACK], BF16, name="w_grouped%d" % z, align_bytes=64)
+            nc.vector.tensor_copy(
+                out=grouped[:].rearrange("p (c i) t -> p c t i", i=4),
+                in_=raw[z][:].rearrange("p t (c i) -> p c t i", i=4),
+            )
+            return grouped
+
+        def quantise_weight(z, grouped):
+            codes = const.tile([P, D_OUT], U32, name="w_codes%d" % z, align_bytes=64)
+            scales = const.tile([P, D_OUT], U8, name="w_scales%d" % z, align_bytes=64)
+            nc.vector.quantize_mx(
+                out=codes[:].bitcast(FP8X4), scales=scales[:], in_=grouped[:].rearrange("p c t -> p (c t)")
+            )
+            return codes, scales
+
+        fold_of, trig_of, x_grouped_of, x_quantised_of = {}, {}, {}, {}
+
+        def first_fold(t, tables):
+            if t not in fold_of:
+                fold_of[t] = fold_pool.tile([P, N_TRIG, P], F32, name="fold", tag="fold")
+            for i in tables:
+                nc.scalar.activation(
+                    out=fold_of[t][:, i, :], in_=frac0[:, i % N_FT, :], func=ACT.Abs,
+                    bias=shifts[:, t, i : i + 1],
+                )
+
+        def second_fold(t, tables):
             nc.scalar.activation(
-                out=tables_of[t][1][:, tiles, :], in_=frac_of[t][:, tiles, :], func=ACT.Sin,
-                scale=(2 * half - 1) * 2.0 * PI,
+                out=fold_of[t][:, tables, :], in_=fold_of[t][:, tables, :], func=ACT.Abs,
+                bias=minus_half[:, 0:1],
             )
 
-        def distance(t):
-            dist = angle_pool.tile(table_shape, F32, name="dist", tag="dist")
-            nc.scalar.activation(out=dist[:], in_=frac_of[t][:], func=ACT.Abs)
-            dist_of[t] = dist
-
-        def cosine(t):
+        def sines(t):
+            trig_of[t] = trig_pool.tile([P, N_TRIG, P], F32, name="trig", tag="trig")
             nc.scalar.activation(
-                out=tables_of[t][0][:], in_=dist_of[t][:], func=ACT.Sin, scale=-2.0 * PI,
-                bias=half_pi[:, 0:1],
+                out=trig_of[t][:, 0:HALF_FT, :], in_=fold_of[t][:, 0:HALF_FT, :], func=ACT.Sin,
+                scale=-2.0 * PI, bias=half_pi[:, 0:1],
+            )
+            nc.scalar.activation(
+                out=trig_of[t][:, HALF_FT:N_FT, :], in_=fold_of[t][:, HALF_FT:N_FT, :], func=ACT.Sin,
+                scale=2.0 * PI, bias=minus_half_pi[:, 0:1],
+            )
+
+        def cosines(t):
+            nc.scalar.activation(
+                out=trig_of[t][:, N_FT:N_TRIG, :], in_=fold_of[t][:, N_FT:N_TRIG, :], func=ACT.Sin,
+                scale=2.0 * PI, bias=minus_half_pi[:, 0:1],
             )
 
         def turn_x(t, first):
@@ -188,7 +206,8 @@ def tile_ropemultiheadattention_pa_t_kernel(tc, x, Wq, bq, Wk, bk, out_0, out_1)
                 words = xin[:, t, first + b, :].bitcast(F32)
                 for u in range(2):
                     nc.tensor.transpose(out=xt[:, b, u, :], in_=words[:, u * P : (u + 1) * P], identity=ident[:])
-            nc.scalar.copy(
+            copy = nc.vector.tensor_copy if t == 0 else nc.scalar.copy
+            copy(
                 out=x_grouped_of[t][:, first * P : (first + 2) * P, :].rearrange("w (b p) u -> w b p u", b=2),
                 in_=xt[:].rearrange("w b u p -> w b p u"),
             )
@@ -204,19 +223,20 @@ def tile_ropemultiheadattention_pa_t_kernel(tc, x, Wq, bq, Wk, bk, out_0, out_1)
             x_quantised_of[t] = (codes, scales)
 
         def prepare(t, part):
-            if part == 0:
-                turn_x(t, 0)
-            elif part == 1:
-                turn_x(t, 2)
+            if part < 2:
+                turn_x(t, 2 * part)
+                first_fold(t, range(HALF_FT * part, HALF_FT * (part + 1)))
             elif part == 2:
                 quantise_x(t)
-                sine(t, 0)
+                first_fold(t, range(N_FT, N_TRIG))
             elif part == 3:
-                sine(t, 1)
+                second_fold(t, slice(0, N_FT))
             elif part == 4:
-                distance(t)
+                second_fold(t, slice(N_FT, N_TRIG))
             elif part == 5:
-                cosine(t)
+                sines(t)
+            elif part == 6:
+                cosines(t)
 
         banks_of, products_of, stage_of = {}, {}, {}
         by_sequence = [P, BATCH, P]
@@ -229,13 +249,15 @@ def tile_ropemultiheadattention_pa_t_kernel(tc, x, Wq, bq, Wk, bk, out_0, out_1)
         def project(k):
             t, z, f = where(k)
             x_codes, x_scales = x_quantised_of[t]
+            w_codes, w_scales = weights[z]
             banks = []
             for h in range(2):
+                features = slice((f + h * HALF_FT) * P, (f + h * HALF_FT + 1) * P)
                 bank = mx_psum.tile([P, TOKENS], F32, name="bank", tag="bank")
                 nc.tensor.matmul_mx(
                     out=bank[:],
-                    lhsT=w_codes[z][:, f, h, :].bitcast(FP8X4),
-                    lhsT_scale=w_scales[z][:, f, h, :],
+                    lhsT=w_codes[:, features].bitcast(FP8X4),
+                    lhsT_scale=w_scales[:, features],
                     rhs=x_codes[:].bitcast(FP8X4),
                     rhs_scale=x_scales[:],
                     start=True,
@@ -256,20 +278,16 @@ def tile_ropemultiheadattention_pa_t_kernel(tc, x, Wq, bq, Wk, bk, out_0, out_1)
 
         def rotate(k):
             t, z, f = where(k)
-            cos_t, sin_t = tables_of[t]
+            trig = trig_of[t]
             own = prod_pool.tile([P, 2, TOKENS], F32, name="own", tag="own")
             other = prod_pool.tile([P, 2, TOKENS], F32, name="other", tag="other")
             for h in range(2):
                 tile_here = f + h * HALF_FT
                 tile_there = f + (1 - h) * HALF_FT
                 bias_col = bias[:, z * N_FT + tile_here : z * N_FT + tile_here + 1]
-                product(own[:, h, :], banks_of[k][h], bias_col, cos_t[:, tile_here, :])
-                product(other[:, 1 - h, :], banks_of[k][h], bias_col, sin_t[:, tile_there, :])
+                product(own[:, h, :], banks_of[k][h], bias_col, trig[:, N_FT + tile_here, :])
+                product(other[:, 1 - h, :], banks_of[k][h], bias_col, trig[:, tile_there, :])
             products_of[k] = (own, other)
-
-        def add_upper(k):
-            own, other = products_of[k]
-            nc.gpsimd.tensor_tensor(out=own[:, 1, :], in0=own[:, 1, :], in1=other[:, 1, :], op=ALU.add)
 
         def sum_and_turn(k):
             t, z, f = where(k)
@@ -281,15 +299,15 @@ def tile_ropemultiheadattention_pa_t_kernel(tc, x, Wq, bq, Wk, bk, out_0, out_1)
                 sums = sum_psum.tile([P, 2, 2, P], F32, name="sums", tag="sums")
                 for b in range(2):
                     tokens = slice((first + b) * P, (first + b + 1) * P)
-                    nc.tensor.matmul(
-                        out=sums[:, b, 0, :], lhsT=own[:, 0, tokens], rhs=ident[:],
-                        is_transpose=True, start=True, stop=False,
-                    )
-                    nc.tensor.matmul(
-                        out=sums[:, b, 0, :], lhsT=other[:, 0, tokens], rhs=ident[:],
-                        is_transpose=True, start=False, stop=True,
-                    )
-                    nc.tensor.transpose(out=sums[:, b, 1, :], in_=own[:, 1, tokens], identity=ident[:])
+                    for h in range(2):
+                        nc.tensor.matmul(
+                            out=sums[:, b, h, :], lhsT=own[:, h, tokens], rhs=ident[:],
+                            is_transpose=True, start=True, stop=False,
+                        )
+                        nc.tensor.matmul(
+                            out=sums[:, b, h, :], lhsT=other[:, h, tokens], rhs=ident[:],
+                            is_transpose=True, start=False, stop=True,
+                        )
                 nc.scalar.copy(
                     out=stage[:, first : first + 2, :].rearrange("p b (h c) -> p b h c", h=2)[
                         :, :, :, f * P : (f + 1) * P
@@ -300,40 +318,29 @@ def tile_ropemultiheadattention_pa_t_kernel(tc, x, Wq, bq, Wk, bk, out_0, out_1)
                 for b in range(BATCH):
                     nc.sync.dma_start(out=outs[z][b, t * P : (t + 1) * P, :], in_=stage[:, b, :])
 
-        for part in range(ANGLE_PARTS):
-            angles(0, part, nc.vector)
-        for part in range(ANGLE_PARTS):
-            angles(1, part, nc.gpsimd)
-        for part in range(PAIRS_PER_BLOCK):
-            prepare(0, part)
-            if part == 1:
-                group_weight(0, 0)
-        quantise_weight(0, 0)
+        prepare(0, 0)
+        prepare(0, 1)
+        grouped_q = group_weight(0)
+        prepare(0, 2)
+        weights = [quantise_weight(0, grouped_q)]
         project(0)
+        for part in range(3, PAIRS_PER_BLOCK):
+            prepare(0, part)
         bias_rows_f32 = const.tile([P, P], F32, name="bias_rows_f32")
         nc.vector.tensor_copy(out=bias_rows_f32[:], in_=bias_rows[:])
         bias_cols = sum_psum.tile([P, P], F32, name="bias_cols", tag="sums")
         nc.tensor.transpose(out=bias_cols[:], in_=bias_rows_f32[:], identity=ident[:])
         bias = const.tile([P, 2 * N_FT], F32, name="bias")
         nc.vector.tensor_copy(out=bias[:], in_=bias_cols[:, 0 : 2 * N_FT])
-        group_weight(0, 1)
-        quantise_weight(0, 1)
+        weights.append(quantise_weight(1, group_weight(1)))
 
-        for k in range(N_PAIRS + 2):
+        for k in range(N_PAIRS + 1):
             if k + 1 < N_PAIRS:
                 project(k + 1)
             if k < N_PAIRS:
                 rotate(k)
-            if k + 2 < PAIRS_PER_BLOCK:
-                z, f = divmod(k + 2, HALF_FT)
-                group_weight(z, f)
-                quantise_weight(z, f)
-            if 1 <= k <= N_PAIRS:
-                add_upper(k - 1)
-            if k >= 2:
-                sum_and_turn(k - 2)
+            if k >= 1:
+                sum_and_turn(k - 1)
             t, part = divmod(k, PAIRS_PER_BLOCK)
             if t + 1 < N_BLOCKS:
                 prepare(t + 1, part)
-            if t + 2 < N_BLOCKS and part < ANGLE_PARTS:
-                angles(t + 2, part, nc.gpsimd)

from contextlib import ExitStack

import concourse.masks as masks
import concourse.mybir as mybir

F32 = mybir.dt.float32
BF16 = mybir.dt.bfloat16
U32 = mybir.dt.uint32
U8 = mybir.dt.uint8
FP8X4 = mybir.dt.float8_e4m3fn_x4
ALU = mybir.AluOpType
ACT = mybir.ActivationFunctionType

P = 128
PACK = 4
BATCH, SEQ, D_IN, D_OUT = 4, 1024, 512, 1024
ROPE_BASE = 10000.0
PI = 3.141592653589793
assert D_IN == P * PACK

N_BLOCKS = SEQ // P
TOKENS = BATCH * P
N_FT = D_OUT // P
HALF_FT = N_FT // 2
PAIRS_PER_BLOCK = 2 * HALF_FT
N_PAIRS = N_BLOCKS * PAIRS_PER_BLOCK
N_TRIG = 2 * N_FT

FREQ_STEP = ROPE_BASE ** (-2.0 / D_OUT)
ROUND_MAGIC = 12582912.0

FLOPS = 2 * BATCH * SEQ * D_IN * 2 * D_OUT


def tile_ropemultiheadattention_pa_t_kernel(tc, x, Wq, bq, Wk, bk, out_0, out_1):
    nc = tc.nc
    outs = (out_0, out_1)
    with ExitStack() as ctx:
        ctx.enter_context(tc.manual_schedule())
        const = ctx.enter_context(tc.tile_pool(name="const", bufs=1))
        xq_pool = ctx.enter_context(tc.tile_pool(name="xq", bufs=2))
        fold_pool = ctx.enter_context(tc.tile_pool(name="fold", bufs=1))
        trig_pool = ctx.enter_context(tc.tile_pool(name="trig", bufs=2))
        prod_pool = ctx.enter_context(tc.tile_pool(name="prod", bufs=3))
        stage_pool = ctx.enter_context(tc.tile_pool(name="stage", bufs=3))
        mx_psum = ctx.enter_context(tc.psum_pool(name="mx_psum", bufs=4))
        sum_psum = ctx.enter_context(tc.psum_pool(name="sum_psum", bufs=3))
        xt_psum = ctx.enter_context(tc.psum_pool(name="xt_psum", bufs=1))

        xin = const.tile([P, N_BLOCKS, BATCH, D_IN], BF16, name="xin")

        def load_x(t):
            nc.sync.dma_start(
                out=xin[:, t, :, :], in_=x[:, t * P : (t + 1) * P, :].rearrange("b p k -> p b k")
            )

        def load_weight(w, label):
            raw = const.tile([P, PACK, D_OUT], BF16, name="raw_" + label)
            for u in range(2):
                nc.sync.dma_start(
                    out=raw[:, 2 * u : 2 * u + 2, :],
                    in_=w[u * 2 * P : (u + 1) * 2 * P, :].rearrange("(q e) c -> q e c", e=2),
                )
            return raw

        bias_rows = const.tile([P, P], BF16, name="bias_rows")
        nc.vector.memset(bias_rows[:], 0.0)
        load_x(0)
        raw = [load_weight(Wq, "q")]
        nc.sync.dma_start(out=bias_rows[0:N_FT, :], in_=bq.rearrange("(r c) -> r c", c=P))
        nc.sync.dma_start(out=bias_rows[N_FT : 2 * N_FT, :], in_=bk.rearrange("(r c) -> r c", c=P))
        raw.append(load_weight(Wk, "k"))
        for t in range(1, N_BLOCKS):
            load_x(t)

        ident = const.tile([P, P], F32, name="ident")
        masks.make_identity(nc, ident[:])

        pos = const.tile([P, P], F32, name="pos")
        nc.vector.memset(pos[:, 0:1], 0.0)
        w = 1
        while w < P:
            nc.vector.tensor_scalar_add(out=pos[:, w : 2 * w], in0=pos[:, 0:w], scalar1=float(w))
            w *= 2

        step_row = const.tile([P, P], F32, name="step_row")
        nc.vector.memset(step_row[:, 0:2], 1.0)
        w = 2
        while w < P:
            nc.vector.tensor_scalar_mul(
                out=step_row[:, w : 2 * w], in0=step_row[:, 0:w], scalar1=FREQ_STEP ** (w // 2)
            )
            w *= 2

        minus_half = const.tile([P, 1], F32, name="minus_half")
        nc.vector.memset(minus_half[:], -0.5)
        half_pi = const.tile([P, 1], F32, name="half_pi")
        nc.vector.tensor_scalar_mul(out=half_pi[:], in0=minus_half[:], scalar1=-PI)
        minus_half_pi = const.tile([P, 1], F32, name="minus_half_pi")
        nc.vector.tensor_scalar_mul(out=minus_half_pi[:], in0=minus_half[:], scalar1=PI)
        warm = const.tile([P, 1], F32, name="warm")
        nc.scalar.activation(out=warm[:], in_=half_pi[:], func=ACT.Sin)

        step_col = sum_psum.tile([P, P], F32, name="step_col", tag="sums")
        nc.tensor.transpose(out=step_col[:], in_=step_row[:], identity=ident[:])
        turns = const.tile([P, N_FT], F32, name="turns")
        nc.vector.tensor_scalar_mul(
            out=turns[:, 0:1], in0=step_col[:, 0:1], scalar1=1.0 / (2.0 * PI)
        )
        w = 1
        while w < N_FT:
            nc.vector.tensor_scalar_mul(
                out=turns[:, w : 2 * w], in0=turns[:, 0:w], scalar1=FREQ_STEP ** (w * P // 2)
            )
            w *= 2

        def nearest_whole_removed(out, value, scratch):
            nc.vector.tensor_scalar(
                out=scratch, in0=value, scalar1=ROUND_MAGIC, scalar2=ROUND_MAGIC,
                op0=ALU.add, op1=ALU.subtract,
            )
            nc.vector.tensor_tensor(out=out, in0=value, in1=scratch, op=ALU.subtract)

        table_shape = [P, N_FT, P]
        angle0 = const.tile(table_shape, F32, name="angle0")
        nc.vector.tensor_tensor(
            out=angle0[:],
            in0=pos[:].unsqueeze(1).to_broadcast(table_shape),
            in1=turns[:].unsqueeze(2).to_broadcast(table_shape),
            op=ALU.mult,
        )
        whole0 = const.tile(table_shape, F32, name="whole0")
        frac0 = const.tile(table_shape, F32, name="frac0")
        nearest_whole_removed(frac0[:], angle0[:], whole0[:])

        block_shape = [P, N_BLOCKS, N_FT]
        block_turns = const.tile([P, N_FT], F32, name="block_turns")
        nc.vector.tensor_scalar_mul(out=block_turns[:], in0=turns[:], scalar1=float(P))
        block_angle = const.tile(block_shape, F32, name="block_angle")
        nc.vector.tensor_tensor(
            out=block_angle[:],
            in0=pos[:, 0:N_BLOCKS].unsqueeze(2).to_broadcast(block_shape),
            in1=block_turns[:].unsqueeze(1).to_broadcast(block_shape),
            op=ALU.mult,
        )
        block_whole = const.tile(block_shape, F32, name="block_whole")
        shifts = const.tile([P, N_BLOCKS, N_TRIG], F32, name="shifts")
        nearest_whole_removed(shifts[:, :, N_FT:N_TRIG], block_angle[:], block_whole[:])
        nc.vector.tensor_scalar_add(out=shifts[:, :, 0:N_FT], in0=shifts[:, :, N_FT:N_TRIG], scalar1=-0.25)

        def group_weight(z):
            grouped = const.tile([P, D_OUT, PACK], BF16, name="w_grouped%d" % z, align_bytes=64)
            nc.vector.tensor_copy(
                out=grouped[:].rearrange("p (c i) t -> p c t i", i=4),
                in_=raw[z][:].rearrange("p t (c i) -> p c t i", i=4),
            )
            return grouped

        def quantise_weight(z, grouped):
            codes = const.tile([P, D_OUT], U32, name="w_codes%d" % z, align_bytes=64)
            scales = const.tile([P, D_OUT], U8, name="w_scales%d" % z, align_bytes=64)
            nc.vector.quantize_mx(
                out=codes[:].bitcast(FP8X4), scales=scales[:], in_=grouped[:].rearrange("p c t -> p (c t)")
            )
            return codes, scales

        fold_of, trig_of, x_grouped_of, x_quantised_of = {}, {}, {}, {}

        def first_fold(t, tables):
            if t not in fold_of:
                fold_of[t] = fold_pool.tile([P, N_TRIG, P], F32, name="fold", tag="fold")
            for i in tables:
                nc.scalar.activation(
                    out=fold_of[t][:, i, :], in_=frac0[:, i % N_FT, :], func=ACT.Abs,
                    bias=shifts[:, t, i : i + 1],
                )

        def second_fold(t, tables):
            nc.scalar.activation(
                out=fold_of[t][:, tables, :], in_=fold_of[t][:, tables, :], func=ACT.Abs,
                bias=minus_half[:, 0:1],
            )

        def sines(t):
            trig_of[t] = trig_pool.tile([P, N_TRIG, P], F32, name="trig", tag="trig")
            nc.scalar.activation(
                out=trig_of[t][:, 0:HALF_FT, :], in_=fold_of[t][:, 0:HALF_FT, :], func=ACT.Sin,
                scale=-2.0 * PI, bias=half_pi[:, 0:1],
            )
            nc.scalar.activation(
                out=trig_of[t][:, HALF_FT:N_FT, :], in_=fold_of[t][:, HALF_FT:N_FT, :], func=ACT.Sin,
                scale=2.0 * PI, bias=minus_half_pi[:, 0:1],
            )

        def cosines(t):
            nc.scalar.activation(
                out=trig_of[t][:, N_FT:N_TRIG, :], in_=fold_of[t][:, N_FT:N_TRIG, :], func=ACT.Sin,
                scale=2.0 * PI, bias=minus_half_pi[:, 0:1],
            )

        def turn_x(t, first):
            if first == 0:
                x_grouped_of[t] = xq_pool.tile([P, TOKENS, 2], F32, name="x_grouped", tag="x_grouped", align_bytes=64)
            xt = xt_psum.tile([P, 2, 2, P], F32, name="xt", tag="xt")
            for b in range(2):
                words = xin[:, t, first + b, :].bitcast(F32)
                for u in range(2):
                    nc.tensor.transpose(out=xt[:, b, u, :], in_=words[:, u * P : (u + 1) * P], identity=ident[:])
            copy = nc.vector.tensor_copy if t == 0 else nc.scalar.copy
            copy(
                out=x_grouped_of[t][:, first * P : (first + 2) * P, :].rearrange("w (b p) u -> w b p u", b=2),
                in_=xt[:].rearrange("w b u p -> w b p u"),
            )

        def quantise_x(t):
            codes = xq_pool.tile([P, TOKENS], U32, name="x_codes", tag="x_codes", align_bytes=64)
            scales = xq_pool.tile([P, TOKENS], U8, name="x_scales", tag="x_scales", align_bytes=64)
            nc.vector.quantize_mx(
                out=codes[:].bitcast(FP8X4),
                scales=scales[:],
                in_=x_grouped_of[t][:].rearrange("w c u -> w (c u)").bitcast(BF16),
            )
            x_quantised_of[t] = (codes, scales)

        def prepare(t, part):
            if part < 2:
                turn_x(t, 2 * part)
                first_fold(t, range(HALF_FT * part, HALF_FT * (part + 1)))
            elif part == 2:
                quantise_x(t)
                first_fold(t, range(N_FT, N_TRIG))
            elif part == 3:
                second_fold(t, slice(0, N_FT))
            elif part == 4:
                second_fold(t, slice(N_FT, N_TRIG))
            elif part == 5:
                sines(t)
            elif part == 6:
                cosines(t)

        banks_of, products_of, stage_of = {}, {}, {}
        by_sequence = [P, BATCH, P]

        def where(k):
            t, rest = divmod(k, PAIRS_PER_BLOCK)
            z, f = divmod(rest, HALF_FT)
            return t, z, f

        def project(k):
            t, z, f = where(k)
            x_codes, x_scales = x_quantised_of[t]
            w_codes, w_scales = weights[z]
            banks = []
            for h in range(2):
                features = slice((f + h * HALF_FT) * P, (f + h * HALF_FT + 1) * P)
                bank = mx_psum.tile([P, TOKENS], F32, name="bank", tag="bank")
                nc.tensor.matmul_mx(
                    out=bank[:],
                    lhsT=w_codes[:, features].bitcast(FP8X4),
                    lhsT_scale=w_scales[:, features],
                    rhs=x_codes[:].bitcast(FP8X4),
                    rhs_scale=x_scales[:],
                    start=True,
                    stop=True,
                )
                banks.append(bank)
            banks_of[k] = banks

        def product(out, bank, bias_col, table):
            nc.vector.scalar_tensor_tensor(
                out=out.rearrange("f (b p) -> f b p", b=BATCH),
                in0=bank[:].rearrange("f (b p) -> f b p", b=BATCH),
                scalar=bias_col,
                in1=table.unsqueeze(1).to_broadcast(by_sequence),
                op0=ALU.add,
                op1=ALU.mult,
            )

        def rotate(k):
            t, z, f = where(k)
            trig = trig_of[t]
            own = prod_pool.tile([P, 2, TOKENS], F32, name="own", tag="own")
            other = prod_pool.tile([P, 2, TOKENS], F32, name="other", tag="other")
            for h in range(2):
                tile_here = f + h * HALF_FT
                tile_there = f + (1 - h) * HALF_FT
                bias_col = bias[:, z * N_FT + tile_here : z * N_FT + tile_here + 1]
                product(own[:, h, :], banks_of[k][h], bias_col, trig[:, N_FT + tile_here, :])
                product(other[:, 1 - h, :], banks_of[k][h], bias_col, trig[:, tile_there, :])
            products_of[k] = (own, other)

        def sum_and_turn(k):
            t, z, f = where(k)
            own, other = products_of[k]
            if f == 0:
                stage_of[(t, z)] = stage_pool.tile([P, BATCH, D_OUT], F32, name="stage", tag="stage")
            stage = stage_of[(t, z)]
            for first in range(0, BATCH, 2):
                sums = sum_psum.tile([P, 2, 2, P], F32, name="sums", tag="sums")
                for b in range(2):
                    tokens = slice((first + b) * P, (first + b + 1) * P)
                    for h in range(2):
                        nc.tensor.matmul(
                            out=sums[:, b, h, :], lhsT=own[:, h, tokens], rhs=ident[:],
                            is_transpose=True, start=True, stop=False,
                        )
                        nc.tensor.matmul(
                            out=sums[:, b, h, :], lhsT=other[:, h, tokens], rhs=ident[:],
                            is_transpose=True, start=False, stop=True,
                        )
                nc.scalar.copy(
                    out=stage[:, first : first + 2, :].rearrange("p b (h c) -> p b h c", h=2)[
                        :, :, :, f * P : (f + 1) * P
                    ],
                    in_=sums[:],
                )
            if f == HALF_FT - 1:
                for b in range(BATCH):
                    nc.sync.dma_start(out=outs[z][b, t * P : (t + 1) * P, :], in_=stage[:, b, :])

        prepare(0, 0)
        prepare(0, 1)
        grouped_q = group_weight(0)
        prepare(0, 2)
        weights = [quantise_weight(0, grouped_q)]
        project(0)
        for part in range(3, PAIRS_PER_BLOCK):
            prepare(0, part)
        bias_rows_f32 = const.tile([P, P], F32, name="bias_rows_f32")
        nc.vector.tensor_copy(out=bias_rows_f32[:], in_=bias_rows[:])
        bias_cols = sum_psum.tile([P, P], F32, name="bias_cols", tag="sums")
        nc.tensor.transpose(out=bias_cols[:], in_=bias_rows_f32[:], identity=ident[:])
        bias = const.tile([P, 2 * N_FT], F32, name="bias")
        nc.vector.tensor_copy(out=bias[:], in_=bias_cols[:, 0 : 2 * N_FT])
        weights.append(quantise_weight(1, group_weight(1)))

        for k in range(N_PAIRS + 1):
            if k + 1 < N_PAIRS:
                project(k + 1)
            if k < N_PAIRS:
                rotate(k)
            if k >= 1:
                sum_and_turn(k - 1)
            t, part = divmod(k, PAIRS_PER_BLOCK)
            if t + 1 < N_BLOCKS:
                prepare(t + 1, part)
